import numpy as np
import ml_dtypes


def mxq(x, axis, fmt="e4m3"):
    dtype, down = {"e4m3": (ml_dtypes.float8_e4m3fn, 7), "e5m2": (ml_dtypes.float8_e5m2, 14)}[fmt]
    v = np.moveaxis(np.asarray(x, np.float32).astype(ml_dtypes.bfloat16).astype(np.float64), axis, -1)
    blocks = v.reshape(v.shape[:-1] + (-1, 32))
    amax = np.abs(blocks).max(-1, keepdims=True)
    byte = np.maximum(np.where(amax > 0, np.frexp(amax)[1] - 1 + 127, 0) - down, 1)
    scale = np.exp2(byte - 127.0)
    codes = (blocks / scale).astype(np.float32).astype(dtype).astype(np.float64)
    return np.moveaxis((codes * scale).reshape(v.shape), -1, axis)


WIDE = False


def mx_kscale(k):
    if not WIDE:
        return np.ones(k)
    levels = np.array([30, -30])
    if k % 512:
        return np.exp2(np.random.permutation(np.resize(levels, k // 32))).repeat(32)
    a = np.empty((k // 512, 16))
    for p in range(k // 512):
        a[p, :8] = np.random.permutation(np.resize(levels, 8))
        for g in range(8):
            far = levels[np.abs(levels - a[p, g]) >= 10]
            a[p, g + 8] = far[np.random.randint(len(far))]
    return np.exp2(a.ravel()).repeat(32)


BF16 = ml_dtypes.bfloat16


def bf(x):
    return np.asarray(x, np.float32).astype(BF16)


def f64(x):
    return np.asarray(x).astype(np.float64)


N, I, O = 8192, 512, 128


def setup_inputs():
    s = mx_kscale(I)
    mask = np.tile(np.array([0.0, 0.0, 1.0, 1.0]), I // 4)
    gd = mask + 0.1 * (1.0 - mask)
    gs = (1.0 - mask) + 0.1 * mask
    x = np.random.standard_normal((N, I)) * s
    wd = np.random.standard_normal((O, I)) * gd / np.sqrt(I) / s
    ws = np.random.standard_normal((O, I)) * gs / np.sqrt(I) / s
    return {"x": bf(x), "W_dense": bf(wd), "W_sparse": bf(ws)}


def reference(x, W_dense, W_sparse):
    xq = mxq(f64(x), 1, "e5m2")
    out_dense = xq @ mxq(f64(W_dense), 1, "e4m3").T
    out_sparse = xq @ mxq(f64(W_sparse), 1, "e4m3").T
    return out_dense + out_sparse

@@ -1,0 +1,187 @@
+from contextlib import ExitStack
+
+import concourse.mybir as mybir
+from concourse.masks import make_identity
+
+TOKENS, K, OUT = 8192, 512, 128
+FLOPS = 2 * 2 * TOKENS * K * OUT
+
+F32 = mybir.dt.float32
+BF16 = mybir.dt.bfloat16
+U32 = mybir.dt.uint32
+U8 = mybir.dt.uint8
+E5M2X4 = mybir.dt.float8_e5m2_x4
+E4M3X4 = mybir.dt.float8_e4m3fn_x4
+
+P = 128
+HALF = 16
+GROUP = 8
+CHUNK = 4
+PAIR = 2
+GROUPS = TOKENS // (P * GROUP)
+BANKS = 8
+STAGE_SLOTS = 4
+
+
+def spans(widths):
+    starts = [sum(widths[:i]) for i in range(len(widths))]
+    return list(zip(starts, widths))
+
+
+def load_widths(g):
+    if g == 0:
+        return (PAIR, PAIR, CHUNK)
+    if g <= 2:
+        return (CHUNK, CHUNK)
+    return (GROUP,)
+
+
+def tile_myinterleavedmodule_t_kernel(tc, x, W_dense, W_sparse, out):
+    nc = tc.nc
+    x_rows = x.rearrange("(g p j) k -> g p j k", p=P, j=GROUP)
+    out_rows = out.rearrange("(g p j) o -> g p j o", p=P, j=GROUP)
+
+    with ExitStack() as ctx:
+        keep = ctx.enter_context(tc.tile_pool(name="keep", bufs=1))
+        psum = ctx.enter_context(tc.psum_pool(name="psum", bufs=1))
+        ctx.enter_context(tc.manual_schedule())
+
+        taken = {"bank": 0, "halves": 0, "grouped": 0, "codes": 0}
+
+        def slot(kind, count):
+            name = "%s%d" % (kind, taken[kind] % count)
+            taken[kind] = taken[kind] + 1
+            return name
+
+        ident = keep.tile([P, P], F32, name="ident")
+        make_identity(nc, ident[:])
+
+        w_raw = keep.tile([P, 2, K], BF16, name="w_raw")
+        nc.sync.dma_start(out=w_raw[:, 0, :], in_=W_dense)
+        nc.sync.dma_start(out=w_raw[:, 1, :], in_=W_sparse)
+        x_raw = {}
+        for g in range(GROUPS):
+            for j0, n in spans(load_widths(g)):
+                raw = keep.tile([P, n, K], BF16, name="x_raw_%d_%d" % (g, j0))
+                nc.sync.dma_start(out=raw[:], in_=x_rows[g, :, j0 : j0 + n, :])
+                for j in range(n):
+                    x_raw[g, j0 + j] = (raw, j)
+
+        def split_halves(raw, n):
+            halves = keep.tile([P, 2, n, K // 2], BF16, name=slot("halves", STAGE_SLOTS))
+            nc.vector.tensor_copy(
+                out=halves[:].rearrange("p u j (b i) -> p u (j b) i", i=HALF),
+                in_=raw.rearrange("p j (b u i) -> p u (j b) i", u=2, i=HALF),
+            )
+            return halves
+
+        def transpose_pair(sources):
+            bank = psum.tile([P, 2, PAIR * P], F32, name=slot("bank", BANKS))
+            for s, (halves, j) in enumerate(sources):
+                for u in range(2):
+                    nc.tensor.transpose(
+                        bank[:, u, s * P : (s + 1) * P], halves[:, u, j, :].bitcast(F32), ident[:]
+                    )
+            return bank
+
+        def copy_on(engine, dst, src):
+            if engine == "vector":
+                nc.vector.tensor_copy(out=dst, in_=src)
+            else:
+                nc.scalar.copy(out=dst, in_=src)
+
+        def interleave(engine, bank, grouped):
+            copy_on(
+                engine,
+                grouped.bitcast(F32).rearrange("p (c u) -> p c u", u=2),
+                bank[:].rearrange("p u c -> p c u"),
+            )
+
+        x_halves = {}
+
+        def split_x(g, j0, n):
+            raw, j_raw = x_raw[g, j0]
+            halves = split_halves(raw[:, j_raw : j_raw + n, :], n)
+            for j in range(n):
+                x_halves[g, j0 + j] = (halves, j)
+
+        x_grouped = {}
+
+        def transpose_group(g, engines):
+            banks = [
+                transpose_pair([x_halves[g, j0 + s] for s in range(PAIR)])
+                for j0 in range(0, GROUP, PAIR)
+            ]
+            for c in range(GROUP // CHUNK):
+                grouped = keep.tile(
+                    [P, CHUNK * K], BF16, name=slot("grouped", STAGE_SLOTS), align_bytes=64
+                )
+                for h in range(CHUNK // PAIR):
+                    b = c * (CHUNK // PAIR) + h
+                    interleave(engines[b], banks[b], grouped[:, h * PAIR * K : (h + 1) * PAIR * K])
+                x_grouped[g, c] = grouped
+
+        x_mx = {}
+
+        def quantize_x(g, c):
+            name = slot("codes", STAGE_SLOTS)
+            x_codes = keep.tile([P, CHUNK * P], U32, name="x_" + name, align_bytes=64)
+            x_scales = keep.tile([P, CHUNK * P], U8, name="x_scales_" + name, align_bytes=64)
+            nc.vector.quantize_mx(
+                out=x_codes[:].bitcast(E5M2X4), scales=x_scales[:], in_=x_grouped[g, c][:]
+            )
+            x_mx[g, c] = (x_codes, x_scales)
+
+        def multiply(g, j0, n):
+            acc = psum.tile([P, n, OUT], F32, name=slot("bank", BANKS))
+            for j in range(j0, j0 + n):
+                x_codes, x_scales = x_mx[g, j // CHUNK]
+                cols = slice((j % CHUNK) * P, (j % CHUNK + 1) * P)
+                for m in range(2):
+                    w_cols = slice(m * OUT, (m + 1) * OUT)
+                    nc.tensor.matmul_mx(
+                        out=acc[:, j - j0, :],
+                        lhsT=x_codes[:, cols].bitcast(E5M2X4),
+                        lhsT_scale=x_scales[:, cols],
+                        rhs=w_codes[:, w_cols].bitcast(E4M3X4),
+                        rhs_scale=w_scales[:, w_cols],
+                        start=(m == 0),
+                        stop=(m == 1),
+                    )
+            return acc
+
+        w_halves = split_halves(w_raw[:], 2)
+        for j0, n in spans(load_widths(0)):
+            split_x(0, j0, n)
+        w_bank = transpose_pair([(w_halves, m) for m in range(2)])
+        w_grouped = keep.tile([P, 2 * K], BF16, name="w_grouped", align_bytes=64)
+        interleave("scalar", w_bank, w_grouped[:])
+        w_codes = keep.tile([P, 2 * OUT], U32, name="w_codes", align_bytes=64)
+        w_scales = keep.tile([P, 2 * OUT], U8, name="w_scales", align_bytes=64)
+        nc.vector.quantize_mx(out=w_codes[:].bitcast(E4M3X4), scales=w_scales[:], in_=w_grouped[:])
+
+        last = GROUPS - 1
+        for g in range(GROUPS):
+            if g < last:
+                split_x(g + 1, 0, CHUNK)
+                transpose_group(g, ["scalar"] * 4)
+            else:
+                transpose_group(g, ["vector", "scalar"] * 2)
+            quantize_x(g, 0)
+            if g < last:
+                split_x(g + 1, CHUNK, CHUNK)
+            if g > 0:
+                result = keep.tile([P, GROUP, OUT], F32, name="result_%d" % (g - 1))
+                accs = [multiply(g - 1, j0, CHUNK) for j0 in (0, CHUNK)]
+                copy_on("vector" if g < last else "scalar", result[:, :CHUNK, :], accs[0][:])
+            quantize_x(g, 1)
+            if g > 0:
+                copy_on("scalar", result[:, CHUNK:, :], accs[1][:])
+                nc.sync.dma_start(out=out_rows[g - 1], in_=result[:])
+
+        tail = spans((CHUNK, PAIR, PAIR))
+        accs = [multiply(last, j0, n) for j0, n in tail]
+        for (j0, n), acc, engine in zip(tail, accs, ("vector", "scalar", "vector")):
+            result = keep.tile([P, n, OUT], F32, name="result_tail_%d" % j0)
+            copy_on(engine, result[:], acc[:])
+            nc.sync.dma_start(out=out_rows[last, :, j0 : j0 + n, :], in_=result[:])

@@ -20,7 +20,11 @@ CHUNK = 4
 PAIR = 2
 GROUPS = TOKENS // (P * GROUP)
 BANKS = 8
-STAGE_SLOTS = 4
+CHUNKS = TOKENS // (P * CHUNK)
+STAGE_SLOTS = 6
+AHEAD = 2
+WHOLE_LOADS_FROM = 4
+WHOLE_STORES_UNTIL = 5
 
 
 def spans(widths):
@@ -30,8 +34,8 @@ def spans(widths):
 
 def load_widths(g):
     if g == 0:
-        return (PAIR, PAIR, CHUNK)
-    if g <= 2:
+        return (PAIR,) * (GROUP // PAIR)
+    if g < WHOLE_LOADS_FROM:
         return (CHUNK, CHUNK)
     return (GROUP,)
 
@@ -57,15 +61,16 @@ def tile_myinterleavedmodule_t_kernel(tc, x, W_dense, W_sparse, out):
         make_identity(nc, ident[:])
 
         w_raw = keep.tile([P, 2, K], BF16, name="w_raw")
-        nc.sync.dma_start(out=w_raw[:, 0, :], in_=W_dense)
-        nc.sync.dma_start(out=w_raw[:, 1, :], in_=W_sparse)
         x_raw = {}
         for g in range(GROUPS):
             for j0, n in spans(load_widths(g)):
                 raw = keep.tile([P, n, K], BF16, name="x_raw_%d_%d" % (g, j0))
                 nc.sync.dma_start(out=raw[:], in_=x_rows[g, :, j0 : j0 + n, :])
                 for j in range(n):
-                    x_raw[g, j0 + j] = (raw, j)
+                    x_raw[g * GROUP + j0 + j] = (raw, j)
+                if g == 0 and j0 == 0:
+                    nc.sync.dma_start(out=w_raw[:, 0, :], in_=W_dense)
+                    nc.sync.dma_start(out=w_raw[:, 1, :], in_=W_sparse)
 
         def split_halves(raw, n):
             halves = keep.tile([P, 2, n, K // 2], BF16, name=slot("halves", STAGE_SLOTS))
@@ -99,89 +104,130 @@ def tile_myinterleavedmodule_t_kernel(tc, x, W_dense, W_sparse, out):
 
         x_halves = {}
 
-        def split_x(g, j0, n):
-            raw, j_raw = x_raw[g, j0]
+        def split_x(t0, n):
+            raw, j_raw = x_raw[t0]
             halves = split_halves(raw[:, j_raw : j_raw + n, :], n)
             for j in range(n):
-                x_halves[g, j0 + j] = (halves, j)
+                x_halves[t0 + j] = (halves, j)
+
+        def split_chunk(c):
+            if c < CHUNKS:
+                split_x(c * CHUNK, CHUNK)
+
+        def transpose_x(t0):
+            return transpose_pair([x_halves[t0 + s] for s in range(PAIR)])
 
         x_grouped = {}
 
-        def transpose_group(g, engines):
-            banks = [
-                transpose_pair([x_halves[g, j0 + s] for s in range(PAIR)])
-                for j0 in range(0, GROUP, PAIR)
-            ]
-            for c in range(GROUP // CHUNK):
-                grouped = keep.tile(
+        def interleave_x(t0, bank):
+            c, j = divmod(t0, CHUNK)
+            if j == 0:
+                x_grouped[c] = keep.tile(
                     [P, CHUNK * K], BF16, name=slot("grouped", STAGE_SLOTS), align_bytes=64
                 )
-                for h in range(CHUNK // PAIR):
-                    b = c * (CHUNK // PAIR) + h
-                    interleave(engines[b], banks[b], grouped[:, h * PAIR * K : (h + 1) * PAIR * K])
-                x_grouped[g, c] = grouped
+            engine = "vector" if j > 0 and c + AHEAD >= CHUNKS else "scalar"
+            interleave(engine, bank, x_grouped[c][:, j * K : (j + PAIR) * K])
+
+        def pieces(c):
+            n = PAIR if c in (0, CHUNKS - 1) else CHUNK
+            return [(j, n) for j in range(0, CHUNK, n)]
 
         x_mx = {}
 
-        def quantize_x(g, c):
+        def quantize_x(c):
             name = slot("codes", STAGE_SLOTS)
             x_codes = keep.tile([P, CHUNK * P], U32, name="x_" + name, align_bytes=64)
             x_scales = keep.tile([P, CHUNK * P], U8, name="x_scales_" + name, align_bytes=64)
-            nc.vector.quantize_mx(
-                out=x_codes[:].bitcast(E5M2X4), scales=x_scales[:], in_=x_grouped[g, c][:]
-            )
-            x_mx[g, c] = (x_codes, x_scales)
+            for j, n in pieces(c):
+                cols = slice(j * P, (j + n) * P)
+                nc.vector.quantize_mx(
+                    out=x_codes[:, cols].bitcast(E5M2X4),
+                    scales=x_scales[:, cols],
+                    in_=x_grouped[c][:, j * K : (j + n) * K],
+                )
+            x_mx[c] = (x_codes, x_scales)
 
-        def multiply(g, j0, n):
-            acc = psum.tile([P, n, OUT], F32, name=slot("bank", BANKS))
-            for j in range(j0, j0 + n):
-                x_codes, x_scales = x_mx[g, j // CHUNK]
-                cols = slice((j % CHUNK) * P, (j % CHUNK + 1) * P)
-                for m in range(2):
-                    w_cols = slice(m * OUT, (m + 1) * OUT)
-                    nc.tensor.matmul_mx(
-                        out=acc[:, j - j0, :],
-                        lhsT=x_codes[:, cols].bitcast(E5M2X4),
-                        lhsT_scale=x_scales[:, cols],
-                        rhs=w_codes[:, w_cols].bitcast(E4M3X4),
-                        rhs_scale=w_scales[:, w_cols],
-                        start=(m == 0),
-                        stop=(m == 1),
+        def multiply(c):
+            x_codes, x_scales = x_mx[c]
+            accs = []
+            for j0, n in pieces(c):
+                acc = psum.tile([P, n, OUT], F32, name=slot("bank", BANKS))
+                for j in range(j0, j0 + n):
+                    cols = slice(j * P, (j + 1) * P)
+                    for m in range(2):
+                        w_cols = slice(m * OUT, (m + 1) * OUT)
+                        nc.tensor.matmul_mx(
+                            out=acc[:, j - j0, :],
+                            lhsT=x_codes[:, cols].bitcast(E5M2X4),
+                            lhsT_scale=x_scales[:, cols],
+                            rhs=w_codes[:, w_cols].bitcast(E4M3X4),
+                            rhs_scale=w_scales[:, w_cols],
+                            start=(m == 0),
+                            stop=(m == 1),
+                        )
+                accs.append(acc)
+            return accs
+
+        results = {}
+
+        def emit(c, accs, engines):
+            for (j0, n), acc, engine in zip(pieces(c), accs, engines):
+                g, j = divmod(c * CHUNK + j0, GROUP)
+                if j == 0:
+                    results[g] = keep.tile([P, GROUP, OUT], F32, name="result_%d" % g)
+                copy_on(engine, results[g][:, j : j + n, :], acc[:])
+                if g >= WHOLE_STORES_UNTIL:
+                    nc.sync.dma_start(
+                        out=out_rows[g, :, j : j + n, :], in_=results[g][:, j : j + n, :]
                     )
-            return acc
+                elif j + n == GROUP:
+                    nc.sync.dma_start(out=out_rows[g], in_=results[g][:])
 
+        split_x(0, PAIR)
         w_halves = split_halves(w_raw[:], 2)
-        for j0, n in spans(load_widths(0)):
-            split_x(0, j0, n)
+        for t0 in range(PAIR, GROUP, PAIR):
+            split_x(t0, PAIR)
+        first_bank = transpose_x(0)
         w_bank = transpose_pair([(w_halves, m) for m in range(2)])
+        banks = [transpose_x(t0) for t0 in range(PAIR, GROUP, PAIR)]
+        interleave_x(0, first_bank)
         w_grouped = keep.tile([P, 2 * K], BF16, name="w_grouped", align_bytes=64)
         interleave("scalar", w_bank, w_grouped[:])
+        for t0, bank in zip(range(PAIR, GROUP, PAIR), banks):
+            interleave_x(t0, bank)
         w_codes = keep.tile([P, 2 * OUT], U32, name="w_codes", align_bytes=64)
         w_scales = keep.tile([P, 2 * OUT], U8, name="w_scales", align_bytes=64)
         nc.vector.quantize_mx(out=w_codes[:].bitcast(E4M3X4), scales=w_scales[:], in_=w_grouped[:])
+        quantize_x(0)
+        split_chunk(2)
+        split_chunk(3)
+        emit(0, multiply(0), ("scalar", "scalar"))
+        quantize_x(1)
 
-        last = GROUPS - 1
-        for g in range(GROUPS):
-            if g < last:
-                split_x(g + 1, 0, CHUNK)
-                transpose_group(g, ["scalar"] * 4)
-            else:
-                transpose_group(g, ["vector", "scalar"] * 2)
-            quantize_x(g, 0)
-            if g < last:
-                split_x(g + 1, CHUNK, CHUNK)
-            if g > 0:
-                result = keep.tile([P, GROUP, OUT], F32, name="result_%d" % (g - 1))
-                accs = [multiply(g - 1, j0, CHUNK) for j0 in (0, CHUNK)]
-                copy_on("vector" if g < last else "scalar", result[:, :CHUNK, :], accs[0][:])
-            quantize_x(g, 1)
-            if g > 0:
-                copy_on("scalar", result[:, CHUNK:, :], accs[1][:])
-                nc.sync.dma_start(out=out_rows[g - 1], in_=result[:])
+        def transpose_chunks(chunks):
+            starts = [t0 for c in chunks for t0 in range(c * CHUNK, (c + 1) * CHUNK, PAIR)]
+            banks = [transpose_x(t0) for t0 in starts]
+            for t0, bank in zip(starts, banks):
+                interleave_x(t0, bank)
 
-        tail = spans((CHUNK, PAIR, PAIR))
-        accs = [multiply(last, j0, n) for j0, n in tail]
-        for (j0, n), acc, engine in zip(tail, accs, ("vector", "scalar", "vector")):
-            result = keep.tile([P, n, OUT], F32, name="result_tail_%d" % j0)
-            copy_on(engine, result[:], acc[:])
-            nc.sync.dma_start(out=out_rows[last, :, j0 : j0 + n, :], in_=result[:])
+        split_chunk(4)
+        transpose_chunks([2])
+        quantize_x(2)
+
+        for c in range(3, CHUNKS - 1, 2):
+            split_chunk(c + AHEAD)
+            transpose_chunks([c, c + 1])
+            quantize_x(c)
+            split_chunk(c + 1 + AHEAD)
+            accs = [multiply(c - 2), multiply(c - 1)]
+            emit(c - 2, accs[0], ["scalar"])
+            quantize_x(c + 1)
+            emit(c - 1, accs[1], ["vector" if c + 1 + AHEAD < CHUNKS else "scalar"])
+
+        last = CHUNKS - 1
+        transpose_chunks([last])
+        accs = [multiply(last - 2), multiply(last - 1)]
+        emit(last - 2, accs[0], ["scalar"])
+        quantize_x(last)
+        emit(last - 1, accs[1], ["scalar"])
+        emit(last, multiply(last), ("scalar", "vector"))

@@ -15,16 +15,15 @@ E4M3X4 = mybir.dt.float8_e4m3fn_x4
 
 P = 128
 HALF = 16
-GROUP = 8
 CHUNK = 4
 PAIR = 2
-GROUPS = TOKENS // (P * GROUP)
+TILES = TOKENS // P
+CHUNKS = TILES // CHUNK
 BANKS = 8
-CHUNKS = TOKENS // (P * CHUNK)
 STAGE_SLOTS = 6
 AHEAD = 2
-WHOLE_LOADS_FROM = 4
-WHOLE_STORES_UNTIL = 5
+LOAD_CHUNKS = (1, 1) + (2,) * 7
+STORE_CHUNKS = (7, 4, 2, 2, 1)
 
 
 def spans(widths):
@@ -32,18 +31,10 @@ def spans(widths):
     return list(zip(starts, widths))
 
 
-def load_widths(g):
-    if g == 0:
-        return (PAIR,) * (GROUP // PAIR)
-    if g < WHOLE_LOADS_FROM:
-        return (CHUNK, CHUNK)
-    return (GROUP,)
-
-
 def tile_myinterleavedmodule_t_kernel(tc, x, W_dense, W_sparse, out):
     nc = tc.nc
-    x_rows = x.rearrange("(g p j) k -> g p j k", p=P, j=GROUP)
-    out_rows = out.rearrange("(g p j) o -> g p j o", p=P, j=GROUP)
+    x_rows = x.rearrange("(p j) k -> p j k", p=P)
+    out_rows = out.rearrange("(p j) o -> p j o", p=P)
 
     with ExitStack() as ctx:
         keep = ctx.enter_context(tc.tile_pool(name="keep", bufs=1))
@@ -62,15 +53,15 @@ def tile_myinterleavedmodule_t_kernel(tc, x, W_dense, W_sparse, out):
 
         w_raw = keep.tile([P, 2, K], BF16, name="w_raw")
         x_raw = {}
-        for g in range(GROUPS):
-            for j0, n in spans(load_widths(g)):
-                raw = keep.tile([P, n, K], BF16, name="x_raw_%d_%d" % (g, j0))
-                nc.sync.dma_start(out=raw[:], in_=x_rows[g, :, j0 : j0 + n, :])
-                for j in range(n):
-                    x_raw[g * GROUP + j0 + j] = (raw, j)
-                if g == 0 and j0 == 0:
-                    nc.sync.dma_start(out=w_raw[:, 0, :], in_=W_dense)
-                    nc.sync.dma_start(out=w_raw[:, 1, :], in_=W_sparse)
+        for c0, count in spans(LOAD_CHUNKS):
+            t0, n = c0 * CHUNK, count * CHUNK
+            raw = keep.tile([P, n, K], BF16, name="x_raw_%d" % c0)
+            nc.sync.dma_start(out=raw[:], in_=x_rows[:, t0 : t0 + n, :])
+            for j in range(n):
+                x_raw[t0 + j] = (raw, j)
+            if c0 == 0:
+                nc.sync.dma_start(out=w_raw[:, 0, :], in_=W_dense)
+                nc.sync.dma_start(out=w_raw[:, 1, :], in_=W_sparse)
 
         def split_halves(raw, n):
             halves = keep.tile([P, 2, n, K // 2], BF16, name=slot("halves", STAGE_SLOTS))
@@ -95,11 +86,10 @@ def tile_myinterleavedmodule_t_kernel(tc, x, W_dense, W_sparse, out):
             else:
                 nc.scalar.copy(out=dst, in_=src)
 
-        def interleave(engine, bank, grouped):
-            copy_on(
-                engine,
-                grouped.bitcast(F32).rearrange("p (c u) -> p c u", u=2),
-                bank[:].rearrange("p u c -> p c u"),
+        def interleave(bank, grouped):
+            nc.scalar.copy(
+                out=grouped.bitcast(F32).rearrange("p (c u) -> p c u", u=2),
+                in_=bank[:].rearrange("p u c -> p c u"),
             )
 
         x_halves = {}
@@ -125,8 +115,7 @@ def tile_myinterleavedmodule_t_kernel(tc, x, W_dense, W_sparse, out):
                 x_grouped[c] = keep.tile(
                     [P, CHUNK * K], BF16, name=slot("grouped", STAGE_SLOTS), align_bytes=64
                 )
-            engine = "vector" if j > 0 and c + AHEAD >= CHUNKS else "scalar"
-            interleave(engine, bank, x_grouped[c][:, j * K : (j + PAIR) * K])
+            interleave(bank, x_grouped[c][:, j * K : (j + PAIR) * K])
 
         def pieces(c):
             n = PAIR if c in (0, CHUNKS - 1) else CHUNK
@@ -169,40 +158,21 @@ def tile_myinterleavedmodule_t_kernel(tc, x, W_dense, W_sparse, out):
             return accs
 
         results = {}
+        for c0, count in spans(STORE_CHUNKS):
+            result = keep.tile([P, count * CHUNK, OUT], F32, name="result_%d" % c0)
+            for c in range(c0, c0 + count):
+                results[c] = (result, c0, count)
 
-        def emit(c, accs, engines):
-            for (j0, n), acc, engine in zip(pieces(c), accs, engines):
-                g, j = divmod(c * CHUNK + j0, GROUP)
-                if j == 0:
-                    results[g] = keep.tile([P, GROUP, OUT], F32, name="result_%d" % g)
-                copy_on(engine, results[g][:, j : j + n, :], acc[:])
-                if g >= WHOLE_STORES_UNTIL:
-                    nc.sync.dma_start(
-                        out=out_rows[g, :, j : j + n, :], in_=results[g][:, j : j + n, :]
-                    )
-                elif j + n == GROUP:
-                    nc.sync.dma_start(out=out_rows[g], in_=results[g][:])
-
-        split_x(0, PAIR)
-        w_halves = split_halves(w_raw[:], 2)
-        for t0 in range(PAIR, GROUP, PAIR):
-            split_x(t0, PAIR)
-        first_bank = transpose_x(0)
-        w_bank = transpose_pair([(w_halves, m) for m in range(2)])
-        banks = [transpose_x(t0) for t0 in range(PAIR, GROUP, PAIR)]
-        interleave_x(0, first_bank)
-        w_grouped = keep.tile([P, 2 * K], BF16, name="w_grouped", align_bytes=64)
-        interleave("scalar", w_bank, w_grouped[:])
-        for t0, bank in zip(range(PAIR, GROUP, PAIR), banks):
-            interleave_x(t0, bank)
-        w_codes = keep.tile([P, 2 * OUT], U32, name="w_codes", align_bytes=64)
-        w_scales = keep.tile([P, 2 * OUT], U8, name="w_scales", align_bytes=64)
-        nc.vector.quantize_mx(out=w_codes[:].bitcast(E4M3X4), scales=w_scales[:], in_=w_grouped[:])
-        quantize_x(0)
-        split_chunk(2)
-        split_chunk(3)
-        emit(0, multiply(0), ("scalar", "scalar"))
-        quantize_x(1)
+        def emit(c, accs):
+            result, c0, count = results[c]
+            for (j0, n), acc in zip(pieces(c), accs):
+                j = (c - c0) * CHUNK + j0
+                on_vector = (c > 0 and c % 2 == 0) or (c == CHUNKS - 1 and j0 > 0)
+                copy_on("vector" if on_vector else "scalar", result[:, j : j + n, :], acc[:])
+            if c == c0 + count - 1:
+                nc.sync.dma_start(
+                    out=out_rows[:, c0 * CHUNK : (c0 + count) * CHUNK, :], in_=result[:]
+                )
 
         def transpose_chunks(chunks):
             starts = [t0 for c in chunks for t0 in range(c * CHUNK, (c + 1) * CHUNK, PAIR)]
@@ -210,24 +180,40 @@ def tile_myinterleavedmodule_t_kernel(tc, x, W_dense, W_sparse, out):
             for t0, bank in zip(starts, banks):
                 interleave_x(t0, bank)
 
-        split_chunk(4)
-        transpose_chunks([2])
-        quantize_x(2)
+        split_x(0, PAIR)
+        w_halves = split_halves(w_raw[:], 2)
+        split_x(PAIR, PAIR)
+        split_chunk(1)
+        first_bank = transpose_x(0)
+        w_bank = transpose_pair([(w_halves, m) for m in range(2)])
+        starts = range(PAIR, 2 * CHUNK, PAIR)
+        banks = [transpose_x(t0) for t0 in starts]
+        interleave_x(0, first_bank)
+        w_grouped = keep.tile([P, 2 * K], BF16, name="w_grouped", align_bytes=64)
+        interleave(w_bank, w_grouped[:])
+        for t0, bank in zip(starts, banks):
+            interleave_x(t0, bank)
+        w_codes = keep.tile([P, 2 * OUT], U32, name="w_codes", align_bytes=64)
+        w_scales = keep.tile([P, 2 * OUT], U8, name="w_scales", align_bytes=64)
+        nc.vector.quantize_mx(out=w_codes[:].bitcast(E4M3X4), scales=w_scales[:], in_=w_grouped[:])
+        quantize_x(0)
+        split_chunk(2)
+        split_chunk(3)
+        emit(0, multiply(0))
+        quantize_x(1)
 
-        for c in range(3, CHUNKS - 1, 2):
-            split_chunk(c + AHEAD)
-            transpose_chunks([c, c + 1])
-            quantize_x(c)
-            split_chunk(c + 1 + AHEAD)
-            accs = [multiply(c - 2), multiply(c - 1)]
-            emit(c - 2, accs[0], ["scalar"])
-            quantize_x(c + 1)
-            emit(c - 1, accs[1], ["vector" if c + 1 + AHEAD < CHUNKS else "scalar"])
-
-        last = CHUNKS - 1
-        transpose_chunks([last])
-        accs = [multiply(last - 2), multiply(last - 1)]
-        emit(last - 2, accs[0], ["scalar"])
-        quantize_x(last)
-        emit(last - 1, accs[1], ["scalar"])
-        emit(last, multiply(last), ("scalar", "vector"))
+        runs = [([2, 3], [1]), ([4], [2])]
+        runs = runs + [([c, c + 1], [c - 2, c - 1]) for c in range(5, CHUNKS - 1, 2)]
+        runs = runs + [([CHUNKS - 1], [CHUNKS - 3, CHUNKS - 2])]
+        for fresh, ready in runs:
+            split_chunk(fresh[0] + AHEAD)
+            transpose_chunks(fresh)
+            for c in fresh[:-1]:
+                quantize_x(c)
+                split_chunk(c + 1 + AHEAD)
+            accs = [multiply(c) for c in ready]
+            emit(ready[0], accs[0])
+            quantize_x(fresh[-1])
+            for c, acc in zip(ready[1:], accs[1:]):
+                emit(c, acc)
+        emit(CHUNKS - 1, multiply(CHUNKS - 1))

from contextlib import ExitStack

import concourse.mybir as mybir
from concourse.masks import make_identity

TOKENS, K, OUT = 8192, 512, 128
FLOPS = 2 * 2 * TOKENS * K * OUT

F32 = mybir.dt.float32
BF16 = mybir.dt.bfloat16
U32 = mybir.dt.uint32
U8 = mybir.dt.uint8
E5M2X4 = mybir.dt.float8_e5m2_x4
E4M3X4 = mybir.dt.float8_e4m3fn_x4

P = 128
HALF = 16
CHUNK = 4
PAIR = 2
TILES = TOKENS // P
CHUNKS = TILES // CHUNK
BANKS = 8
STAGE_SLOTS = 6
AHEAD = 2
LOAD_CHUNKS = (1, 1) + (2,) * 7
STORE_CHUNKS = (7, 4, 2, 2, 1)


def spans(widths):
    starts = [sum(widths[:i]) for i in range(len(widths))]
    return list(zip(starts, widths))


def tile_myinterleavedmodule_t_kernel(tc, x, W_dense, W_sparse, out):
    nc = tc.nc
    x_rows = x.rearrange("(p j) k -> p j k", p=P)
    out_rows = out.rearrange("(p j) o -> p j o", p=P)

    with ExitStack() as ctx:
        keep = ctx.enter_context(tc.tile_pool(name="keep", bufs=1))
        psum = ctx.enter_context(tc.psum_pool(name="psum", bufs=1))
        ctx.enter_context(tc.manual_schedule())

        taken = {"bank": 0, "halves": 0, "grouped": 0, "codes": 0}

        def slot(kind, count):
            name = "%s%d" % (kind, taken[kind] % count)
            taken[kind] = taken[kind] + 1
            return name

        ident = keep.tile([P, P], F32, name="ident")
        make_identity(nc, ident[:])

        w_raw = keep.tile([P, 2, K], BF16, name="w_raw")
        x_raw = {}
        for c0, count in spans(LOAD_CHUNKS):
            t0, n = c0 * CHUNK, count * CHUNK
            raw = keep.tile([P, n, K], BF16, name="x_raw_%d" % c0)
            nc.sync.dma_start(out=raw[:], in_=x_rows[:, t0 : t0 + n, :])
            for j in range(n):
                x_raw[t0 + j] = (raw, j)
            if c0 == 0:
                nc.sync.dma_start(out=w_raw[:, 0, :], in_=W_dense)
                nc.sync.dma_start(out=w_raw[:, 1, :], in_=W_sparse)

        def split_halves(raw, n):
            halves = keep.tile([P, 2, n, K // 2], BF16, name=slot("halves", STAGE_SLOTS))
            nc.vector.tensor_copy(
                out=halves[:].rearrange("p u j (b i) -> p u (j b) i", i=HALF),
                in_=raw.rearrange("p j (b u i) -> p u (j b) i", u=2, i=HALF),
            )
            return halves

        def transpose_pair(sources):
            bank = psum.tile([P, 2, PAIR * P], F32, name=slot("bank", BANKS))
            for s, (halves, j) in enumerate(sources):
                for u in range(2):
                    nc.tensor.transpose(
                        bank[:, u, s * P : (s + 1) * P], halves[:, u, j, :].bitcast(F32), ident[:]
                    )
            return bank

        def copy_on(engine, dst, src):
            if engine == "vector":
                nc.vector.tensor_copy(out=dst, in_=src)
            else:
                nc.scalar.copy(out=dst, in_=src)

        def interleave(bank, grouped):
            nc.scalar.copy(
                out=grouped.bitcast(F32).rearrange("p (c u) -> p c u", u=2),
                in_=bank[:].rearrange("p u c -> p c u"),
            )

        x_halves = {}

        def split_x(t0, n):
            raw, j_raw = x_raw[t0]
            halves = split_halves(raw[:, j_raw : j_raw + n, :], n)
            for j in range(n):
                x_halves[t0 + j] = (halves, j)

        def split_chunk(c):
            if c < CHUNKS:
                split_x(c * CHUNK, CHUNK)

        def transpose_x(t0):
            return transpose_pair([x_halves[t0 + s] for s in range(PAIR)])

        x_grouped = {}

        def interleave_x(t0, bank):
            c, j = divmod(t0, CHUNK)
            if j == 0:
                x_grouped[c] = keep.tile(
                    [P, CHUNK * K], BF16, name=slot("grouped", STAGE_SLOTS), align_bytes=64
                )
            interleave(bank, x_grouped[c][:, j * K : (j + PAIR) * K])

        def pieces(c):
            n = PAIR if c in (0, CHUNKS - 1) else CHUNK
            return [(j, n) for j in range(0, CHUNK, n)]

        x_mx = {}

        def quantize_x(c):
            name = slot("codes", STAGE_SLOTS)
            x_codes = keep.tile([P, CHUNK * P], U32, name="x_" + name, align_bytes=64)
            x_scales = keep.tile([P, CHUNK * P], U8, name="x_scales_" + name, align_bytes=64)
            for j, n in pieces(c):
                cols = slice(j * P, (j + n) * P)
                nc.vector.quantize_mx(
                    out=x_codes[:, cols].bitcast(E5M2X4),
                    scales=x_scales[:, cols],
                    in_=x_grouped[c][:, j * K : (j + n) * K],
                )
            x_mx[c] = (x_codes, x_scales)

        def multiply(c):
            x_codes, x_scales = x_mx[c]
            accs = []
            for j0, n in pieces(c):
                acc = psum.tile([P, n, OUT], F32, name=slot("bank", BANKS))
                for j in range(j0, j0 + n):
                    cols = slice(j * P, (j + 1) * P)
                    for m in range(2):
                        w_cols = slice(m * OUT, (m + 1) * OUT)
                        nc.tensor.matmul_mx(
                            out=acc[:, j - j0, :],
                            lhsT=x_codes[:, cols].bitcast(E5M2X4),
                            lhsT_scale=x_scales[:, cols],
                            rhs=w_codes[:, w_cols].bitcast(E4M3X4),
                            rhs_scale=w_scales[:, w_cols],
                            start=(m == 0),
                            stop=(m == 1),
                        )
                accs.append(acc)
            return accs

        results = {}
        for c0, count in spans(STORE_CHUNKS):
            result = keep.tile([P, count * CHUNK, OUT], F32, name="result_%d" % c0)
            for c in range(c0, c0 + count):
                results[c] = (result, c0, count)

        def emit(c, accs):
            result, c0, count = results[c]
            for (j0, n), acc in zip(pieces(c), accs):
                j = (c - c0) * CHUNK + j0
                on_vector = (c > 0 and c % 2 == 0) or (c == CHUNKS - 1 and j0 > 0)
                copy_on("vector" if on_vector else "scalar", result[:, j : j + n, :], acc[:])
            if c == c0 + count - 1:
                nc.sync.dma_start(
                    out=out_rows[:, c0 * CHUNK : (c0 + count) * CHUNK, :], in_=result[:]
                )

        def transpose_chunks(chunks):
            starts = [t0 for c in chunks for t0 in range(c * CHUNK, (c + 1) * CHUNK, PAIR)]
            banks = [transpose_x(t0) for t0 in starts]
            for t0, bank in zip(starts, banks):
                interleave_x(t0, bank)

        split_x(0, PAIR)
        w_halves = split_halves(w_raw[:], 2)
        split_x(PAIR, PAIR)
        split_chunk(1)
        first_bank = transpose_x(0)
        w_bank = transpose_pair([(w_halves, m) for m in range(2)])
        starts = range(PAIR, 2 * CHUNK, PAIR)
        banks = [transpose_x(t0) for t0 in starts]
        interleave_x(0, first_bank)
        w_grouped = keep.tile([P, 2 * K], BF16, name="w_grouped", align_bytes=64)
        interleave(w_bank, w_grouped[:])
        for t0, bank in zip(starts, banks):
            interleave_x(t0, bank)
        w_codes = keep.tile([P, 2 * OUT], U32, name="w_codes", align_bytes=64)
        w_scales = keep.tile([P, 2 * OUT], U8, name="w_scales", align_bytes=64)
        nc.vector.quantize_mx(out=w_codes[:].bitcast(E4M3X4), scales=w_scales[:], in_=w_grouped[:])
        quantize_x(0)
        split_chunk(2)
        split_chunk(3)
        emit(0, multiply(0))
        quantize_x(1)

        runs = [([2, 3], [1]), ([4], [2])]
        runs = runs + [([c, c + 1], [c - 2, c - 1]) for c in range(5, CHUNKS - 1, 2)]
        runs = runs + [([CHUNKS - 1], [CHUNKS - 3, CHUNKS - 2])]
        for fresh, ready in runs:
            split_chunk(fresh[0] + AHEAD)
            transpose_chunks(fresh)
            for c in fresh[:-1]:
                quantize_x(c)
                split_chunk(c + 1 + AHEAD)
            accs = [multiply(c) for c in ready]
            emit(ready[0], accs[0])
            quantize_x(fresh[-1])
            for c, acc in zip(ready[1:], accs[1:]):
                emit(c, acc)
        emit(CHUNKS - 1, multiply(CHUNKS - 1))
